import numpy as np
import ml_dtypes

BF16 = ml_dtypes.bfloat16


def bf(x):
    return np.asarray(x, np.float32).astype(BF16)


def f32(x):
    return np.asarray(x, np.float32)


def f64(x):
    return np.asarray(x).astype(np.float64)


def striped(idx):
    return np.tile(idx.reshape(-1, 16).T, (8, 1))


C, S, M, B, H, N = 1024, 256, 128, 8, 16, 128
SC = 0.4


def setup_inputs():
    return {"table": f32(SC * np.random.standard_normal((C, S))), "targ": f32(SC * np.random.standard_normal((C, B))), "w1": bf(np.random.standard_normal((C, M)) / (SC * SC * np.sqrt(C))), "b1": f32(0.1 * np.random.standard_normal((M, 1))), "offs": striped(np.random.permutation(np.tile(np.arange(S), 2))[:N])}


def reference(table, targ, w1, b1, offs):
    idx = offs[:16].T.reshape(-1)
    x = f64(table)[:, idx] * np.repeat(f64(targ), H, axis=1)
    h1 = np.maximum(f64(w1).T @ x + f64(b1), 0.0)
    return np.concatenate([x, h1], axis=0)

@@ -1,0 +1,85 @@
+import concourse.mybir as mybir
+
+F32, BF16, U16 = mybir.dt.float32, mybir.dt.bfloat16, mybir.dt.uint16
+ALU = mybir.AluOpType
+
+P = 128
+C, S, M, B, H, N = 1024, 256, 128, 8, 16, 128
+BLOCKS = C // P
+HALF = BLOCKS // 2
+PAIR = 2
+BURST = 256
+
+FLOPS = 2 * C * M * N
+
+
+def tile_new4_kernel(tc, table, targ, w1, b1, offs, out):
+    nc = tc.nc
+
+    table_blocks = table.rearrange("(p k) s -> p k s", k=BLOCKS)
+    x_blocks = out[0:C, :].rearrange("(p k) j -> p k j", k=BLOCKS)
+
+    with (
+        tc.tile_pool(name="held", bufs=1) as held,
+        tc.psum_pool(name="psum", bufs=1) as psum,
+    ):
+        offsets = held.tile([P, N // 16], U16, name="offsets")
+        nc.sync.dma_start(offsets[:], offs)
+        targets = held.tile([P, BLOCKS * B], F32, name="targets", align_bytes=BURST)
+        nc.scalar.dma_start(targets[:], targ.rearrange("(p k) u -> p (k u)", k=BLOCKS))
+        bias = held.tile([M, 1], F32, name="bias")
+        nc.scalar.dma_start(bias[:], b1)
+
+        windows = [held.tile([P, S], F32, name=f"window{k}", align_bytes=BURST) for k in range(BLOCKS)]
+        nc.sync.dma_start(windows[0][:], table_blocks[:, 0, :])
+        weight_blocks = w1.rearrange("(p k) m -> p k m", k=BLOCKS)
+        weights_of_block = []
+
+        def load_weights(queue, first, count):
+            part = held.tile([P, count, M], BF16, name=f"weights{first}", align_bytes=BURST)
+            queue.dma_start(part[:], weight_blocks[:, first : first + count, :])
+            weights_of_block.extend([part[:, i, :] for i in range(count)])
+
+        load_weights(nc.scalar, 0, HALF)
+        for k in range(1, BLOCKS):
+            nc.sync.dma_start(windows[k][:], table_blocks[:, k, :])
+        load_weights(nc.sync, HALF, PAIR)
+        load_weights(nc.sync, HALF + PAIR, PAIR)
+
+        target_of_entry = [held.tile([P, B, H], F32, name=f"target_of_entry{k}") for k in range(BLOCKS)]
+        for k in range(BLOCKS):
+            nc.scalar.copy(
+                target_of_entry[k][:],
+                targets[:, k * B : (k + 1) * B].unsqueeze(2).to_broadcast([P, B, H]),
+            )
+
+        hidden_sum = psum.tile([M, N], F32, name="hidden_sum")
+        products = held.tile([P, BLOCKS, N], F32, name="products", align_bytes=BURST)
+        for k in range(BLOCKS):
+            x = products[:, k, :]
+            nc.vector.tensor_tensor(
+                x,
+                windows[k][:].indirect(offsets[:]),
+                target_of_entry[k][:].rearrange("p u h -> p (u h)"),
+                ALU.mult,
+            )
+
+            if k % 2 == 1:
+                nc.sync.dma_start(x_blocks[:, k - 1 : k + 1, :], products[:, k - 1 : k + 1, :])
+
+            x_bf16 = held.tile([P, N], BF16, name=f"x_bf16_{k}")
+            if k < BLOCKS - 1:
+                nc.scalar.copy(x_bf16[:], x)
+            else:
+                nc.vector.tensor_copy(x_bf16[:], x)
+            nc.tensor.matmul(
+                hidden_sum[:],
+                weights_of_block[k],
+                x_bf16[:],
+                start=(k == 0),
+                stop=(k == BLOCKS - 1),
+            )
+
+        hidden = held.tile([M, N], F32, name="hidden", align_bytes=BURST)
+        nc.vector.tensor_scalar(hidden[:], hidden_sum[:], bias[:, 0:1], 0.0, ALU.add, ALU.max)
+        nc.scalar.dma_start(out[C : C + M, :], hidden[:])

@@ -6,7 +6,6 @@ ALU = mybir.AluOpType
 P = 128
 C, S, M, B, H, N = 1024, 256, 128, 8, 16, 128
 BLOCKS = C // P
-HALF = BLOCKS // 2
 PAIR = 2
 BURST = 256
 
@@ -40,11 +39,11 @@ def tile_new4_kernel(tc, table, targ, w1, b1, offs, out):
             queue.dma_start(part[:], weight_blocks[:, first : first + count, :])
             weights_of_block.extend([part[:, i, :] for i in range(count)])
 
-        load_weights(nc.scalar, 0, HALF)
+        load_weights(nc.scalar, 0, PAIR)
         for k in range(1, BLOCKS):
             nc.sync.dma_start(windows[k][:], table_blocks[:, k, :])
-        load_weights(nc.sync, HALF, PAIR)
-        load_weights(nc.sync, HALF + PAIR, PAIR)
+        for first in range(PAIR, BLOCKS, PAIR):
+            load_weights(nc.sync, first, PAIR)
 
         target_of_entry = [held.tile([P, B, H], F32, name=f"target_of_entry{k}") for k in range(BLOCKS)]
         for k in range(BLOCKS):

@@ -47,10 +47,11 @@ def tile_new4_kernel(tc, table, targ, w1, b1, offs, out):
 
         target_of_entry = [held.tile([P, B, H], F32, name=f"target_of_entry{k}") for k in range(BLOCKS)]
         for k in range(BLOCKS):
-            nc.scalar.copy(
-                target_of_entry[k][:],
-                targets[:, k * B : (k + 1) * B].unsqueeze(2).to_broadcast([P, B, H]),
-            )
+            target_16_times = targets[:, k * B : (k + 1) * B].unsqueeze(2).to_broadcast([P, B, H])
+            if k == 0:
+                nc.vector.tensor_copy(target_of_entry[k][:], target_16_times)
+            else:
+                nc.scalar.copy(target_of_entry[k][:], target_16_times)
 
         hidden_sum = psum.tile([M, N], F32, name="hidden_sum")
         products = held.tile([P, BLOCKS, N], F32, name="products", align_bytes=BURST)

import concourse.mybir as mybir

F32, BF16, U16 = mybir.dt.float32, mybir.dt.bfloat16, mybir.dt.uint16
ALU = mybir.AluOpType

P = 128
C, S, M, B, H, N = 1024, 256, 128, 8, 16, 128
BLOCKS = C // P
PAIR = 2
BURST = 256

FLOPS = 2 * C * M * N


def tile_new4_kernel(tc, table, targ, w1, b1, offs, out):
    nc = tc.nc

    table_blocks = table.rearrange("(p k) s -> p k s", k=BLOCKS)
    x_blocks = out[0:C, :].rearrange("(p k) j -> p k j", k=BLOCKS)

    with (
        tc.tile_pool(name="held", bufs=1) as held,
        tc.psum_pool(name="psum", bufs=1) as psum,
    ):
        offsets = held.tile([P, N // 16], U16, name="offsets")
        nc.sync.dma_start(offsets[:], offs)
        targets = held.tile([P, BLOCKS * B], F32, name="targets", align_bytes=BURST)
        nc.scalar.dma_start(targets[:], targ.rearrange("(p k) u -> p (k u)", k=BLOCKS))
        bias = held.tile([M, 1], F32, name="bias")
        nc.scalar.dma_start(bias[:], b1)

        windows = [held.tile([P, S], F32, name=f"window{k}", align_bytes=BURST) for k in range(BLOCKS)]
        nc.sync.dma_start(windows[0][:], table_blocks[:, 0, :])
        weight_blocks = w1.rearrange("(p k) m -> p k m", k=BLOCKS)
        weights_of_block = []

        def load_weights(queue, first, count):
            part = held.tile([P, count, M], BF16, name=f"weights{first}", align_bytes=BURST)
            queue.dma_start(part[:], weight_blocks[:, first : first + count, :])
            weights_of_block.extend([part[:, i, :] for i in range(count)])

        load_weights(nc.scalar, 0, PAIR)
        for k in range(1, BLOCKS):
            nc.sync.dma_start(windows[k][:], table_blocks[:, k, :])
        for first in range(PAIR, BLOCKS, PAIR):
            load_weights(nc.sync, first, PAIR)

        target_of_entry = [held.tile([P, B, H], F32, name=f"target_of_entry{k}") for k in range(BLOCKS)]
        for k in range(BLOCKS):
            target_16_times = targets[:, k * B : (k + 1) * B].unsqueeze(2).to_broadcast([P, B, H])
            if k == 0:
                nc.vector.tensor_copy(target_of_entry[k][:], target_16_times)
            else:
                nc.scalar.copy(target_of_entry[k][:], target_16_times)

        hidden_sum = psum.tile([M, N], F32, name="hidden_sum")
        products = held.tile([P, BLOCKS, N], F32, name="products", align_bytes=BURST)
        for k in range(BLOCKS):
            x = products[:, k, :]
            nc.vector.tensor_tensor(
                x,
                windows[k][:].indirect(offsets[:]),
                target_of_entry[k][:].rearrange("p u h -> p (u h)"),
                ALU.mult,
            )

            if k % 2 == 1:
                nc.sync.dma_start(x_blocks[:, k - 1 : k + 1, :], products[:, k - 1 : k + 1, :])

            x_bf16 = held.tile([P, N], BF16, name=f"x_bf16_{k}")
            if k < BLOCKS - 1:
                nc.scalar.copy(x_bf16[:], x)
            else:
                nc.vector.tensor_copy(x_bf16[:], x)
            nc.tensor.matmul(
                hidden_sum[:],
                weights_of_block[k],
                x_bf16[:],
                start=(k == 0),
                stop=(k == BLOCKS - 1),
            )

        hidden = held.tile([M, N], F32, name="hidden", align_bytes=BURST)
        nc.vector.tensor_scalar(hidden[:], hidden_sum[:], bias[:, 0:1], 0.0, ALU.add, ALU.max)
        nc.scalar.dma_start(out[C : C + M, :], hidden[:])
